import numpy as np
import ml_dtypes


def mxq(x, axis, fmt="e4m3"):
    dtype, down = {"e4m3": (ml_dtypes.float8_e4m3fn, 7), "e5m2": (ml_dtypes.float8_e5m2, 14)}[fmt]
    v = np.moveaxis(np.asarray(x, np.float32).astype(ml_dtypes.bfloat16).astype(np.float64), axis, -1)
    blocks = v.reshape(v.shape[:-1] + (-1, 32))
    amax = np.abs(blocks).max(-1, keepdims=True)
    byte = np.maximum(np.where(amax > 0, np.frexp(amax)[1] - 1 + 127, 0) - down, 1)
    scale = np.exp2(byte - 127.0)
    codes = (blocks / scale).astype(np.float32).astype(dtype).astype(np.float64)
    return np.moveaxis((codes * scale).reshape(v.shape), -1, axis)


WIDE = False


def mx_kscale(k):
    if not WIDE:
        return np.ones(k)
    levels = np.array([20, -20, 10, -10, 0])
    a = np.random.permutation(np.resize(levels, k // 512 * 4)).reshape(k // 512, 4)
    idx = np.arange(k)
    return np.exp2(a[idx // 512, idx % 128 // 32])


BF16 = ml_dtypes.bfloat16


def bf(x):
    return np.asarray(x, np.float32).astype(BF16)


def f64(x):
    return np.asarray(x).astype(np.float64)


S, D = 512, 512
HALF = D // 2
BASE = 10000.0


def rope_tables():
    freqs = 1.0 / BASE ** (np.arange(HALF) / HALF)
    ang = np.arange(S)[:, None] * freqs[None, :]
    return np.cos(ang), np.sin(ang)


def rope_interleaved(v):
    cos, sin = rope_tables()
    vp = v.reshape(S, HALF, 2)
    vr, vi = vp[..., 0], vp[..., 1]
    rot = np.stack([vr * cos - vi * sin, vr * sin + vi * cos], axis=-1)
    return rot.reshape(S, D)


def rope_interleaved_back(g):
    cos, sin = rope_tables()
    gp = g.reshape(S, HALF, 2)
    gr, gi = gp[..., 0], gp[..., 1]
    rot = np.stack([gr * cos + gi * sin, gi * cos - gr * sin], axis=-1)
    return rot.reshape(S, D)


def setup_inputs():
    u = np.repeat(mx_kscale(D)[::2], 2)
    x = np.random.standard_normal((S, D))
    w = np.random.standard_normal((D, D)) / np.sqrt(D) / u[:, None]
    g = np.random.standard_normal((S, D)) * np.exp2(np.random.randint(-12, 1, (S, 1))) * 8.0 * u[None, :]
    return {"x": bf(x), "w": bf(w), "grad_out": bf(g)}


def reference(x, w, grad_out):
    gy = rope_interleaved_back(f64(grad_out))
    return mxq(gy, 1, "e5m2") @ mxq(f64(w), 0, "e4m3")

@@ -1,0 +1,190 @@
+import math
+from contextlib import ExitStack
+
+import concourse.mybir as mybir
+from concourse.masks import make_identity
+
+F32 = mybir.dt.float32
+BF16 = mybir.dt.bfloat16
+U32 = mybir.dt.uint32
+U8 = mybir.dt.uint8
+E4M3_X4 = mybir.dt.float8_e4m3fn_x4
+E5M2_X4 = mybir.dt.float8_e5m2_x4
+ALU = mybir.AluOpType
+ACT = mybir.ActivationFunctionType
+
+S = 512
+D = 512
+P = 128
+PACK = 4
+HALF = D // 2
+TILES = S // P
+BASE = 10000.0
+
+SLOW = 144
+assert (S - 1) * BASE ** (-SLOW / HALF) < math.pi
+
+ROUND = 1.5 * 2.0**23
+
+FLOPS = 2 * S * D * D
+BYTES = 2 * D * D + 2 * S * D + 4 * S * D
+
+
+def tile_ropeattention_pa_s_kernel(tc, x, w, grad_out, out):
+    nc = tc.nc
+    with ExitStack() as ctx:
+        keep = ctx.enter_context(tc.tile_pool(name="keep", bufs=1))
+        work = ctx.enter_context(tc.tile_pool(name="work", bufs=2))
+        flipped_pool = ctx.enter_context(tc.psum_pool(name="flipped", bufs=4))
+        acc_pool = ctx.enter_context(tc.psum_pool(name="acc", bufs=4))
+
+        w_rows = keep.tile([P, PACK, D], BF16)
+        nc.sync.dma_start(
+            out=w_rows[:].rearrange("p (u e) n -> p u e n", u=2),
+            in_=w.rearrange("(u p e) n -> p u e n", u=2, e=2),
+        )
+        g_rows = keep.tile([P, TILES, D], BF16)
+        for t in range(TILES):
+            nc.sync.dma_start(out=g_rows[:, t, :], in_=grad_out[t * P : (t + 1) * P, :])
+
+        position = keep.tile([P, TILES], F32)
+        nc.gpsimd.iota(
+            position[:],
+            pattern=[[P, TILES]],
+            base=0,
+            channel_multiplier=1,
+            allow_small_or_imprecise_dtypes=True,
+        )
+        identity = keep.tile([P, P], BF16)
+        make_identity(nc, identity[:])
+
+        freq = keep.tile([P, HALF], F32)
+        nc.vector.memset(freq[:, 0:1], 1.0)
+        have = 1
+        while have < HALF:
+            for d in range(1, 4):
+                nc.vector.tensor_scalar_mul(
+                    out=freq[:, d * have : (d + 1) * have],
+                    in0=freq[:, 0:have],
+                    scalar1=BASE ** (-d * have / HALF),
+                )
+            have *= 4
+
+        one = keep.tile([P, 1], F32)
+        nc.vector.memset(one[:], 1.0)
+        quarter_turn = keep.tile([P, 1], F32)
+        nc.vector.tensor_scalar_mul(out=quarter_turn[:], in0=one[:], scalar1=math.pi / 2)
+        minus_position = keep.tile([P, TILES], F32)
+        nc.vector.tensor_scalar_mul(out=minus_position[:], in0=position[:], scalar1=-1.0)
+        position_turns = keep.tile([P, TILES], F32)
+        nc.vector.tensor_scalar_mul(
+            out=position_turns[:], in0=position[:], scalar1=1.0 / (2.0 * math.pi)
+        )
+
+        cos = keep.tile([P, TILES, HALF], F32)
+        sin = keep.tile([P, TILES, HALF], F32)
+
+        for t in range(TILES):
+            nc.scalar.activation(
+                out=sin[:, t, SLOW:], in_=freq[:, SLOW:], func=ACT.Sin, scale=position[:, t : t + 1]
+            )
+            nc.scalar.activation(
+                out=cos[:, t, SLOW:],
+                in_=freq[:, SLOW:],
+                func=ACT.Sin,
+                scale=minus_position[:, t : t + 1],
+                bias=quarter_turn[:],
+            )
+
+        turns = keep.tile([P, TILES, SLOW], F32)
+        shifted = keep.tile([P, TILES, SLOW], F32)
+        for t in range(TILES):
+            nc.vector.tensor_scalar_mul(
+                out=turns[:, t, :], in0=freq[:, :SLOW], scalar1=position_turns[:, t : t + 1]
+            )
+            nc.vector.tensor_scalar(
+                out=shifted[:, t, :],
+                in0=freq[:, :SLOW],
+                scalar1=position_turns[:, t : t + 1],
+                scalar2=ROUND,
+                op0=ALU.mult,
+                op1=ALU.add,
+            )
+        excess = keep.tile([P, TILES, SLOW], F32)
+        nc.vector.scalar_tensor_tensor(
+            out=excess[:],
+            in0=shifted[:],
+            scalar=ROUND,
+            in1=turns[:],
+            op0=ALU.subtract,
+            op1=ALU.subtract,
+        )
+        nc.scalar.activation(out=sin[:, :, :SLOW], in_=excess[:], func=ACT.Sin, scale=-2.0 * math.pi)
+        size = keep.tile([P, TILES, SLOW], F32)
+        nc.scalar.activation(out=size[:], in_=excess[:], func=ACT.Abs)
+        nc.scalar.activation(
+            out=cos[:, :, :SLOW],
+            in_=size[:],
+            func=ACT.Sin,
+            scale=-2.0 * math.pi,
+            bias=quarter_turn[:],
+        )
+
+        w_grouped = keep.tile([P, D, PACK], BF16, align_bytes=64)
+        nc.vector.tensor_copy(out=w_grouped[:], in_=w_rows[:].rearrange("p q n -> p n q"))
+        w_codes = keep.tile([P, D], U32, align_bytes=64)
+        w_scales = keep.tile([P, D], U8, align_bytes=64)
+        nc.vector.quantize_mx(
+            out=w_codes[:].bitcast(E4M3_X4),
+            scales=w_scales[:],
+            in_=w_grouped[:].rearrange("p n q -> p (n q)"),
+        )
+
+        for t in range(TILES):
+            pairs = g_rows[:, t, :].rearrange("p (i e) -> p i e", e=2)
+            g_even = pairs[:, :, 0]
+            g_odd = pairs[:, :, 1]
+
+            gy = work.tile([P, 2, HALF], BF16)
+            even_cos = work.tile([P, HALF], F32)
+            odd_sin = work.tile([P, HALF], F32)
+            nc.vector.tensor_mul(out=even_cos[:], in0=g_even, in1=cos[:, t, :])
+            nc.vector.tensor_mul(out=odd_sin[:], in0=g_odd, in1=sin[:, t, :])
+            nc.vector.tensor_add(out=gy[:, 0, :], in0=even_cos[:], in1=odd_sin[:])
+            odd_cos = work.tile([P, HALF], F32)
+            even_sin = work.tile([P, HALF], F32)
+            nc.vector.tensor_mul(out=odd_cos[:], in0=g_odd, in1=cos[:, t, :])
+            nc.vector.tensor_mul(out=even_sin[:], in0=g_even, in1=sin[:, t, :])
+            nc.vector.tensor_sub(out=gy[:, 1, :], in0=odd_cos[:], in1=even_sin[:])
+
+            flipped = flipped_pool.tile([P, PACK, P], BF16)
+            for u in range(2):
+                for e in range(2):
+                    nc.tensor.transpose(
+                        out=flipped[:, 2 * u + e, :],
+                        in_=gy[:, e, u * P : (u + 1) * P],
+                        identity=identity[:],
+                    )
+            gy_grouped = work.tile([P, P, PACK], BF16, align_bytes=64)
+            nc.scalar.copy(out=gy_grouped[:], in_=flipped[:].rearrange("p q j -> p j q"))
+            gy_codes = work.tile([P, P], U32, align_bytes=64)
+            gy_scales = work.tile([P, P], U8, align_bytes=64)
+            nc.vector.quantize_mx(
+                out=gy_codes[:].bitcast(E5M2_X4),
+                scales=gy_scales[:],
+                in_=gy_grouped[:].rearrange("p j q -> p (j q)"),
+            )
+
+            acc = acc_pool.tile([P, D], F32)
+            nc.tensor.matmul_mx(
+                out=acc[:],
+                lhsT=gy_codes[:].bitcast(E5M2_X4),
+                lhsT_scale=gy_scales[:],
+                rhs=w_codes[:].bitcast(E4M3_X4),
+                rhs_scale=w_scales[:],
+                start=True,
+                stop=True,
+            )
+            result = work.tile([P, D], F32)
+            nc.scalar.copy(out=result[:], in_=acc[:])
+            nc.sync.dma_start(out=out[t * P : (t + 1) * P, :], in_=result[:])

@@ -33,19 +33,20 @@ BYTES = 2 * D * D + 2 * S * D + 4 * S * D
 def tile_ropeattention_pa_s_kernel(tc, x, w, grad_out, out):
     nc = tc.nc
     with ExitStack() as ctx:
+        ctx.enter_context(tc.manual_schedule())
         keep = ctx.enter_context(tc.tile_pool(name="keep", bufs=1))
-        work = ctx.enter_context(tc.tile_pool(name="work", bufs=2))
-        flipped_pool = ctx.enter_context(tc.psum_pool(name="flipped", bufs=4))
-        acc_pool = ctx.enter_context(tc.psum_pool(name="acc", bufs=4))
+        work = ctx.enter_context(tc.tile_pool(name="work", bufs=TILES))
+        flipped_pool = ctx.enter_context(tc.psum_pool(name="flipped", bufs=TILES))
+        acc_pool = ctx.enter_context(tc.psum_pool(name="acc", bufs=TILES))
 
+        g_rows = keep.tile([P, TILES, D], BF16)
+        for t in range(TILES):
+            nc.sync.dma_start(out=g_rows[:, t, :], in_=grad_out[t * P : (t + 1) * P, :])
         w_rows = keep.tile([P, PACK, D], BF16)
         nc.sync.dma_start(
             out=w_rows[:].rearrange("p (u e) n -> p u e n", u=2),
             in_=w.rearrange("(u p e) n -> p u e n", u=2, e=2),
         )
-        g_rows = keep.tile([P, TILES, D], BF16)
-        for t in range(TILES):
-            nc.sync.dma_start(out=g_rows[:, t, :], in_=grad_out[t * P : (t + 1) * P, :])
 
         position = keep.tile([P, TILES], F32)
         nc.gpsimd.iota(
@@ -55,7 +56,7 @@ def tile_ropeattention_pa_s_kernel(tc, x, w, grad_out, out):
             channel_multiplier=1,
             allow_small_or_imprecise_dtypes=True,
         )
-        identity = keep.tile([P, P], BF16)
+        identity = keep.tile([P, P], F32)
         make_identity(nc, identity[:])
 
         freq = keep.tile([P, HALF], F32)
@@ -70,10 +71,8 @@ def tile_ropeattention_pa_s_kernel(tc, x, w, grad_out, out):
                 )
             have *= 4
 
-        one = keep.tile([P, 1], F32)
-        nc.vector.memset(one[:], 1.0)
         quarter_turn = keep.tile([P, 1], F32)
-        nc.vector.tensor_scalar_mul(out=quarter_turn[:], in0=one[:], scalar1=math.pi / 2)
+        nc.vector.tensor_scalar_mul(out=quarter_turn[:], in0=freq[:, 0:1], scalar1=math.pi / 2)
         minus_position = keep.tile([P, TILES], F32)
         nc.vector.tensor_scalar_mul(out=minus_position[:], in0=position[:], scalar1=-1.0)
         position_turns = keep.tile([P, TILES], F32)
@@ -98,6 +97,8 @@ def tile_ropeattention_pa_s_kernel(tc, x, w, grad_out, out):
 
         turns = keep.tile([P, TILES, SLOW], F32)
         shifted = keep.tile([P, TILES, SLOW], F32)
+        excess = keep.tile([P, TILES, SLOW], F32)
+        size = keep.tile([P, TILES, SLOW], F32)
         for t in range(TILES):
             nc.vector.tensor_scalar_mul(
                 out=turns[:, t, :], in0=freq[:, :SLOW], scalar1=position_turns[:, t : t + 1]
@@ -110,63 +111,82 @@ def tile_ropeattention_pa_s_kernel(tc, x, w, grad_out, out):
                 op0=ALU.mult,
                 op1=ALU.add,
             )
-        excess = keep.tile([P, TILES, SLOW], F32)
-        nc.vector.scalar_tensor_tensor(
-            out=excess[:],
-            in0=shifted[:],
-            scalar=ROUND,
-            in1=turns[:],
-            op0=ALU.subtract,
-            op1=ALU.subtract,
-        )
-        nc.scalar.activation(out=sin[:, :, :SLOW], in_=excess[:], func=ACT.Sin, scale=-2.0 * math.pi)
-        size = keep.tile([P, TILES, SLOW], F32)
-        nc.scalar.activation(out=size[:], in_=excess[:], func=ACT.Abs)
-        nc.scalar.activation(
-            out=cos[:, :, :SLOW],
-            in_=size[:],
-            func=ACT.Sin,
-            scale=-2.0 * math.pi,
-            bias=quarter_turn[:],
-        )
+            nc.vector.scalar_tensor_tensor(
+                out=excess[:, t, :],
+                in0=shifted[:, t, :],
+                scalar=ROUND,
+                in1=turns[:, t, :],
+                op0=ALU.subtract,
+                op1=ALU.subtract,
+            )
+            nc.scalar.activation(
+                out=sin[:, t, :SLOW], in_=excess[:, t, :], func=ACT.Sin, scale=-2.0 * math.pi
+            )
+            nc.scalar.activation(out=size[:, t, :], in_=excess[:, t, :], func=ACT.Abs)
+            nc.scalar.activation(
+                out=cos[:, t, :SLOW],
+                in_=size[:, t, :],
+                func=ACT.Sin,
+                scale=-2.0 * math.pi,
+                bias=quarter_turn[:],
+            )
 
-        w_grouped = keep.tile([P, D, PACK], BF16, align_bytes=64)
-        nc.vector.tensor_copy(out=w_grouped[:], in_=w_rows[:].rearrange("p q n -> p n q"))
         w_codes = keep.tile([P, D], U32, align_bytes=64)
         w_scales = keep.tile([P, D], U8, align_bytes=64)
-        nc.vector.quantize_mx(
-            out=w_codes[:].bitcast(E4M3_X4),
-            scales=w_scales[:],
-            in_=w_grouped[:].rearrange("p n q -> p (n q)"),
-        )
 
-        for t in range(TILES):
+        def quantise_w():
+            w_grouped = keep.tile([P, D, PACK], BF16, align_bytes=64)
+            nc.vector.tensor_copy(out=w_grouped[:], in_=w_rows[:].rearrange("p q n -> p n q"))
+            nc.vector.quantize_mx(
+                out=w_codes[:].bitcast(E4M3_X4),
+                scales=w_scales[:],
+                in_=w_grouped[:].rearrange("p n q -> p (n q)"),
+            )
+
+        def rotate_and_flip(t):
             pairs = g_rows[:, t, :].rearrange("p (i e) -> p i e", e=2)
             g_even = pairs[:, :, 0]
             g_odd = pairs[:, :, 1]
-
-            gy = work.tile([P, 2, HALF], BF16)
             even_cos = work.tile([P, HALF], F32)
             odd_sin = work.tile([P, HALF], F32)
+            odd_cos = work.tile([P, HALF], F32)
+            minus_even_sin = work.tile([P, HALF], F32)
             nc.vector.tensor_mul(out=even_cos[:], in0=g_even, in1=cos[:, t, :])
             nc.vector.tensor_mul(out=odd_sin[:], in0=g_odd, in1=sin[:, t, :])
-            nc.vector.tensor_add(out=gy[:, 0, :], in0=even_cos[:], in1=odd_sin[:])
-            odd_cos = work.tile([P, HALF], F32)
-            even_sin = work.tile([P, HALF], F32)
             nc.vector.tensor_mul(out=odd_cos[:], in0=g_odd, in1=cos[:, t, :])
-            nc.vector.tensor_mul(out=even_sin[:], in0=g_even, in1=sin[:, t, :])
-            nc.vector.tensor_sub(out=gy[:, 1, :], in0=odd_cos[:], in1=even_sin[:])
-
-            flipped = flipped_pool.tile([P, PACK, P], BF16)
-            for u in range(2):
-                for e in range(2):
-                    nc.tensor.transpose(
+            nc.vector.scalar_tensor_tensor(
+                out=minus_even_sin[:],
+                in0=g_even,
+                scalar=-1.0,
+                in1=sin[:, t, :],
+                op0=ALU.mult,
+                op1=ALU.mult,
+            )
+            flipped = flipped_pool.tile([P, PACK, P], F32)
+            for e, (first, second) in enumerate(((even_cos, odd_sin), (odd_cos, minus_even_sin))):
+                for u in range(2):
+                    block = slice(u * P, (u + 1) * P)
+                    nc.tensor.matmul(
                         out=flipped[:, 2 * u + e, :],
-                        in_=gy[:, e, u * P : (u + 1) * P],
-                        identity=identity[:],
+                        lhsT=first[:, block],
+                        rhs=identity[:],
+                        is_transpose=True,
+                        start=True,
+                        stop=False,
+                    )
+                    nc.tensor.matmul(
+                        out=flipped[:, 2 * u + e, :],
+                        lhsT=second[:, block],
+                        rhs=identity[:],
+                        is_transpose=True,
+                        start=False,
+                        stop=True,
                     )
             gy_grouped = work.tile([P, P, PACK], BF16, align_bytes=64)
             nc.scalar.copy(out=gy_grouped[:], in_=flipped[:].rearrange("p q j -> p j q"))
+            return gy_grouped
+
+        def multiply_and_store(t, gy_grouped):
             gy_codes = work.tile([P, P], U32, align_bytes=64)
             gy_scales = work.tile([P, P], U8, align_bytes=64)
             nc.vector.quantize_mx(
@@ -174,7 +194,6 @@ def tile_ropeattention_pa_s_kernel(tc, x, w, grad_out, out):
                 scales=gy_scales[:],
                 in_=gy_grouped[:].rearrange("p j q -> p (j q)"),
             )
-
             acc = acc_pool.tile([P, D], F32)
             nc.tensor.matmul_mx(
                 out=acc[:],
@@ -188,3 +207,11 @@ def tile_ropeattention_pa_s_kernel(tc, x, w, grad_out, out):
             result = work.tile([P, D], F32)
             nc.scalar.copy(out=result[:], in_=acc[:])
             nc.sync.dma_start(out=out[t * P : (t + 1) * P, :], in_=result[:])
+
+        waiting = rotate_and_flip(0)
+        quantise_w()
+        for t in range(1, TILES):
+            rotated = rotate_and_flip(t)
+            multiply_and_store(t - 1, waiting)
+            waiting = rotated
+        multiply_and_store(TILES - 1, waiting)

@@ -40,13 +40,19 @@ def tile_ropeattention_pa_s_kernel(tc, x, w, grad_out, out):
         acc_pool = ctx.enter_context(tc.psum_pool(name="acc", bufs=TILES))
 
         g_rows = keep.tile([P, TILES, D], BF16)
-        for t in range(TILES):
-            nc.sync.dma_start(out=g_rows[:, t, :], in_=grad_out[t * P : (t + 1) * P, :])
         w_rows = keep.tile([P, PACK, D], BF16)
+
+        def load_g(t):
+            nc.sync.dma_start(out=g_rows[:, t, :], in_=grad_out[t * P : (t + 1) * P, :])
+
+        load_g(0)
+        load_g(1)
         nc.sync.dma_start(
             out=w_rows[:].rearrange("p (u e) n -> p u e n", u=2),
             in_=w.rearrange("(u p e) n -> p u e n", u=2, e=2),
         )
+        load_g(2)
+        load_g(3)
 
         position = keep.tile([P, TILES], F32)
         nc.gpsimd.iota(
@@ -82,8 +88,12 @@ def tile_ropeattention_pa_s_kernel(tc, x, w, grad_out, out):
 
         cos = keep.tile([P, TILES, HALF], F32)
         sin = keep.tile([P, TILES, HALF], F32)
+        turns = keep.tile([P, TILES, SLOW], F32)
+        shifted = keep.tile([P, TILES, SLOW], F32)
+        excess = keep.tile([P, TILES, SLOW], F32)
+        size = keep.tile([P, TILES, SLOW], F32)
 
-        for t in range(TILES):
+        def make_tables(t):
             nc.scalar.activation(
                 out=sin[:, t, SLOW:], in_=freq[:, SLOW:], func=ACT.Sin, scale=position[:, t : t + 1]
             )
@@ -94,12 +104,6 @@ def tile_ropeattention_pa_s_kernel(tc, x, w, grad_out, out):
                 scale=minus_position[:, t : t + 1],
                 bias=quarter_turn[:],
             )
-
-        turns = keep.tile([P, TILES, SLOW], F32)
-        shifted = keep.tile([P, TILES, SLOW], F32)
-        excess = keep.tile([P, TILES, SLOW], F32)
-        size = keep.tile([P, TILES, SLOW], F32)
-        for t in range(TILES):
             nc.vector.tensor_scalar_mul(
                 out=turns[:, t, :], in0=freq[:, :SLOW], scalar1=position_turns[:, t : t + 1]
             )
@@ -136,39 +140,43 @@ def tile_ropeattention_pa_s_kernel(tc, x, w, grad_out, out):
 
         def quantise_w():
             w_grouped = keep.tile([P, D, PACK], BF16, align_bytes=64)
-            nc.vector.tensor_copy(out=w_grouped[:], in_=w_rows[:].rearrange("p q n -> p n q"))
+            nc.vector.tensor_copy(
+                out=w_grouped[:].rearrange("p (c i) q -> p c q i", i=4),
+                in_=w_rows[:].rearrange("p q (c i) -> p c q i", i=4),
+            )
             nc.vector.quantize_mx(
                 out=w_codes[:].bitcast(E4M3_X4),
                 scales=w_scales[:],
                 in_=w_grouped[:].rearrange("p n q -> p (n q)"),
             )
 
+        gy_grouped = [None] * TILES
+
         def rotate_and_flip(t):
-            pairs = g_rows[:, t, :].rearrange("p (i e) -> p i e", e=2)
-            g_even = pairs[:, :, 0]
-            g_odd = pairs[:, :, 1]
-            even_cos = work.tile([P, HALF], F32)
-            odd_sin = work.tile([P, HALF], F32)
-            odd_cos = work.tile([P, HALF], F32)
-            minus_even_sin = work.tile([P, HALF], F32)
-            nc.vector.tensor_mul(out=even_cos[:], in0=g_even, in1=cos[:, t, :])
-            nc.vector.tensor_mul(out=odd_sin[:], in0=g_odd, in1=sin[:, t, :])
-            nc.vector.tensor_mul(out=odd_cos[:], in0=g_odd, in1=cos[:, t, :])
+            pairs = g_rows[:, t, :].rearrange("p (i e) -> p e i", e=2)
+            by_sin = work.tile([P, 2, HALF], F32)
+            by_cos = work.tile([P, 2, HALF], F32)
+            nc.vector.tensor_mul(out=by_sin[:, 0, :], in0=pairs[:, 1, :], in1=sin[:, t, :])
             nc.vector.scalar_tensor_tensor(
-                out=minus_even_sin[:],
-                in0=g_even,
+                out=by_sin[:, 1, :],
+                in0=pairs[:, 0, :],
                 scalar=-1.0,
                 in1=sin[:, t, :],
                 op0=ALU.mult,
                 op1=ALU.mult,
             )
+            nc.vector.tensor_mul(
+                out=by_cos[:],
+                in0=pairs,
+                in1=cos[:, t, :].unsqueeze(1).to_broadcast([P, 2, HALF]),
+            )
             flipped = flipped_pool.tile([P, PACK, P], F32)
-            for e, (first, second) in enumerate(((even_cos, odd_sin), (odd_cos, minus_even_sin))):
+            for e in range(2):
                 for u in range(2):
                     block = slice(u * P, (u + 1) * P)
                     nc.tensor.matmul(
                         out=flipped[:, 2 * u + e, :],
-                        lhsT=first[:, block],
+                        lhsT=by_sin[:, e, block],
                         rhs=identity[:],
                         is_transpose=True,
                         start=True,
@@ -176,23 +184,23 @@ def tile_ropeattention_pa_s_kernel(tc, x, w, grad_out, out):
                     )
                     nc.tensor.matmul(
                         out=flipped[:, 2 * u + e, :],
-                        lhsT=second[:, block],
+                        lhsT=by_cos[:, e, block],
                         rhs=identity[:],
                         is_transpose=True,
                         start=False,
                         stop=True,
                     )
-            gy_grouped = work.tile([P, P, PACK], BF16, align_bytes=64)
-            nc.scalar.copy(out=gy_grouped[:], in_=flipped[:].rearrange("p q j -> p j q"))
-            return gy_grouped
+            grouped = work.tile([P, P, PACK], BF16, align_bytes=64)
+            nc.scalar.copy(out=grouped[:], in_=flipped[:].rearrange("p q j -> p j q"))
+            gy_grouped[t] = grouped
 
-        def multiply_and_store(t, gy_grouped):
+        def multiply_and_store(t):
             gy_codes = work.tile([P, P], U32, align_bytes=64)
             gy_scales = work.tile([P, P], U8, align_bytes=64)
             nc.vector.quantize_mx(
                 out=gy_codes[:].bitcast(E5M2_X4),
                 scales=gy_scales[:],
-                in_=gy_grouped[:].rearrange("p j q -> p (j q)"),
+                in_=gy_grouped[t][:].rearrange("p j q -> p (j q)"),
             )
             acc = acc_pool.tile([P, D], F32)
             nc.tensor.matmul_mx(
@@ -208,10 +216,16 @@ def tile_ropeattention_pa_s_kernel(tc, x, w, grad_out, out):
             nc.scalar.copy(out=result[:], in_=acc[:])
             nc.sync.dma_start(out=out[t * P : (t + 1) * P, :], in_=result[:])
 
-        waiting = rotate_and_flip(0)
+        make_tables(0)
+        make_tables(1)
+        rotate_and_flip(0)
+        make_tables(2)
         quantise_w()
-        for t in range(1, TILES):
-            rotated = rotate_and_flip(t)
-            multiply_and_store(t - 1, waiting)
-            waiting = rotated
-        multiply_and_store(TILES - 1, waiting)
+        rotate_and_flip(1)
+        make_tables(3)
+        rotate_and_flip(2)
+        multiply_and_store(0)
+        multiply_and_store(1)
+        rotate_and_flip(3)
+        multiply_and_store(2)
+        multiply_and_store(3)

@@ -42,17 +42,12 @@ def tile_ropeattention_pa_s_kernel(tc, x, w, grad_out, out):
         g_rows = keep.tile([P, TILES, D], BF16)
         w_rows = keep.tile([P, PACK, D], BF16)
 
-        def load_g(t):
+        for t in range(TILES):
             nc.sync.dma_start(out=g_rows[:, t, :], in_=grad_out[t * P : (t + 1) * P, :])
-
-        load_g(0)
-        load_g(1)
         nc.sync.dma_start(
             out=w_rows[:].rearrange("p (u e) n -> p u e n", u=2),
             in_=w.rearrange("(u p e) n -> p u e n", u=2, e=2),
         )
-        load_g(2)
-        load_g(3)
 
         position = keep.tile([P, TILES], F32)
         nc.gpsimd.iota(
@@ -88,22 +83,11 @@ def tile_ropeattention_pa_s_kernel(tc, x, w, grad_out, out):
 
         cos = keep.tile([P, TILES, HALF], F32)
         sin = keep.tile([P, TILES, HALF], F32)
+
         turns = keep.tile([P, TILES, SLOW], F32)
         shifted = keep.tile([P, TILES, SLOW], F32)
         excess = keep.tile([P, TILES, SLOW], F32)
-        size = keep.tile([P, TILES, SLOW], F32)
-
-        def make_tables(t):
-            nc.scalar.activation(
-                out=sin[:, t, SLOW:], in_=freq[:, SLOW:], func=ACT.Sin, scale=position[:, t : t + 1]
-            )
-            nc.scalar.activation(
-                out=cos[:, t, SLOW:],
-                in_=freq[:, SLOW:],
-                func=ACT.Sin,
-                scale=minus_position[:, t : t + 1],
-                bias=quarter_turn[:],
-            )
+        for t in range(TILES):
             nc.vector.tensor_scalar_mul(
                 out=turns[:, t, :], in0=freq[:, :SLOW], scalar1=position_turns[:, t : t + 1]
             )
@@ -115,6 +99,7 @@ def tile_ropeattention_pa_s_kernel(tc, x, w, grad_out, out):
                 op0=ALU.mult,
                 op1=ALU.add,
             )
+        for t in range(TILES):
             nc.vector.scalar_tensor_tensor(
                 out=excess[:, t, :],
                 in0=shifted[:, t, :],
@@ -122,6 +107,19 @@ def tile_ropeattention_pa_s_kernel(tc, x, w, grad_out, out):
                 in1=turns[:, t, :],
                 op0=ALU.subtract,
                 op1=ALU.subtract,
+            )
+
+        size = keep.tile([P, TILES, SLOW], F32)
+        for t in range(TILES):
+            nc.scalar.activation(
+                out=sin[:, t, SLOW:], in_=freq[:, SLOW:], func=ACT.Sin, scale=position[:, t : t + 1]
+            )
+            nc.scalar.activation(
+                out=cos[:, t, SLOW:],
+                in_=freq[:, SLOW:],
+                func=ACT.Sin,
+                scale=minus_position[:, t : t + 1],
+                bias=quarter_turn[:],
             )
             nc.scalar.activation(
                 out=sin[:, t, :SLOW], in_=excess[:, t, :], func=ACT.Sin, scale=-2.0 * math.pi
@@ -135,28 +133,19 @@ def tile_ropeattention_pa_s_kernel(tc, x, w, grad_out, out):
                 bias=quarter_turn[:],
             )
 
-        w_codes = keep.tile([P, D], U32, align_bytes=64)
-        w_scales = keep.tile([P, D], U8, align_bytes=64)
+        w_grouped = keep.tile([P, D, PACK], BF16, align_bytes=64)
+        nc.scalar.copy(
+            out=w_grouped[:].rearrange("p (c i) q -> p c q i", i=4),
+            in_=w_rows[:].rearrange("p q (c i) -> p c q i", i=4),
+        )
 
-        def quantise_w():
-            w_grouped = keep.tile([P, D, PACK], BF16, align_bytes=64)
-            nc.vector.tensor_copy(
-                out=w_grouped[:].rearrange("p (c i) q -> p c q i", i=4),
-                in_=w_rows[:].rearrange("p q (c i) -> p c q i", i=4),
-            )
-            nc.vector.quantize_mx(
-                out=w_codes[:].bitcast(E4M3_X4),
-                scales=w_scales[:],
-                in_=w_grouped[:].rearrange("p n q -> p (n q)"),
-            )
-
-        gy_grouped = [None] * TILES
-
-        def rotate_and_flip(t):
+        gy_grouped = keep.tile([P, TILES, P, PACK], BF16, align_bytes=64)
+        for t in range(TILES):
             pairs = g_rows[:, t, :].rearrange("p (i e) -> p e i", e=2)
             by_sin = work.tile([P, 2, HALF], F32)
             by_cos = work.tile([P, 2, HALF], F32)
             nc.vector.tensor_mul(out=by_sin[:, 0, :], in0=pairs[:, 1, :], in1=sin[:, t, :])
+            nc.vector.tensor_mul(out=by_cos[:, 0, :], in0=pairs[:, 0, :], in1=cos[:, t, :])
             nc.vector.scalar_tensor_tensor(
                 out=by_sin[:, 1, :],
                 in0=pairs[:, 0, :],
@@ -165,11 +154,7 @@ def tile_ropeattention_pa_s_kernel(tc, x, w, grad_out, out):
                 op0=ALU.mult,
                 op1=ALU.mult,
             )
-            nc.vector.tensor_mul(
-                out=by_cos[:],
-                in0=pairs,
-                in1=cos[:, t, :].unsqueeze(1).to_broadcast([P, 2, HALF]),
-            )
+            nc.vector.tensor_mul(out=by_cos[:, 1, :], in0=pairs[:, 1, :], in1=cos[:, t, :])
             flipped = flipped_pool.tile([P, PACK, P], F32)
             for e in range(2):
                 for u in range(2):
@@ -190,42 +175,38 @@ def tile_ropeattention_pa_s_kernel(tc, x, w, grad_out, out):
                         start=False,
                         stop=True,
                     )
-            grouped = work.tile([P, P, PACK], BF16, align_bytes=64)
-            nc.scalar.copy(out=grouped[:], in_=flipped[:].rearrange("p q j -> p j q"))
-            gy_grouped[t] = grouped
+            nc.scalar.copy(out=gy_grouped[:, t], in_=flipped[:].rearrange("p q j -> p j q"))
 
-        def multiply_and_store(t):
-            gy_codes = work.tile([P, P], U32, align_bytes=64)
-            gy_scales = work.tile([P, P], U8, align_bytes=64)
+        w_codes = keep.tile([P, D], U32, align_bytes=64)
+        w_scales = keep.tile([P, D], U8, align_bytes=64)
+        nc.vector.quantize_mx(
+            out=w_codes[:].bitcast(E4M3_X4),
+            scales=w_scales[:],
+            in_=w_grouped[:].rearrange("p n q -> p (n q)"),
+        )
+        gy_codes = keep.tile([P, TILES, P], U32, align_bytes=64)
+        gy_scales = keep.tile([P, TILES, P], U8, align_bytes=64)
+        for t in range(TILES):
             nc.vector.quantize_mx(
-                out=gy_codes[:].bitcast(E5M2_X4),
-                scales=gy_scales[:],
-                in_=gy_grouped[t][:].rearrange("p j q -> p (j q)"),
+                out=gy_codes[:, t, :].bitcast(E5M2_X4),
+                scales=gy_scales[:, t, :],
+                in_=gy_grouped[:, t].rearrange("p j q -> p (j q)"),
             )
+
+        for t in range(TILES):
             acc = acc_pool.tile([P, D], F32)
             nc.tensor.matmul_mx(
                 out=acc[:],
-                lhsT=gy_codes[:].bitcast(E5M2_X4),
-                lhsT_scale=gy_scales[:],
+                lhsT=gy_codes[:, t, :].bitcast(E5M2_X4),
+                lhsT_scale=gy_scales[:, t, :],
                 rhs=w_codes[:].bitcast(E4M3_X4),
                 rhs_scale=w_scales[:],
                 start=True,
                 stop=True,
             )
             result = work.tile([P, D], F32)
-            nc.scalar.copy(out=result[:], in_=acc[:])
+            if t % 2 == 0:
+                nc.scalar.copy(out=result[:], in_=acc[:])
+            else:
+                nc.vector.tensor_copy(out=result[:], in_=acc[:])
             nc.sync.dma_start(out=out[t * P : (t + 1) * P, :], in_=result[:])
-
-        make_tables(0)
-        make_tables(1)
-        rotate_and_flip(0)
-        make_tables(2)
-        quantise_w()
-        rotate_and_flip(1)
-        make_tables(3)
-        rotate_and_flip(2)
-        multiply_and_store(0)
-        multiply_and_store(1)
-        rotate_and_flip(3)
-        multiply_and_store(2)
-        multiply_and_store(3)

@@ -6,6 +6,7 @@ from concourse.masks import make_identity
 
 F32 = mybir.dt.float32
 BF16 = mybir.dt.bfloat16
+I32 = mybir.dt.int32
 U32 = mybir.dt.uint32
 U8 = mybir.dt.uint8
 E4M3_X4 = mybir.dt.float8_e4m3fn_x4
@@ -23,8 +24,6 @@ BASE = 10000.0
 
 SLOW = 144
 assert (S - 1) * BASE ** (-SLOW / HALF) < math.pi
-
-ROUND = 1.5 * 2.0**23
 
 FLOPS = 2 * S * D * D
 BYTES = 2 * D * D + 2 * S * D + 4 * S * D
@@ -72,40 +71,31 @@ def tile_ropeattention_pa_s_kernel(tc, x, w, grad_out, out):
                 )
             have *= 4
 
-        quarter_turn = keep.tile([P, 1], F32)
-        nc.vector.tensor_scalar_mul(out=quarter_turn[:], in0=freq[:, 0:1], scalar1=math.pi / 2)
-        minus_position = keep.tile([P, TILES], F32)
-        nc.vector.tensor_scalar_mul(out=minus_position[:], in0=position[:], scalar1=-1.0)
         position_turns = keep.tile([P, TILES], F32)
         nc.vector.tensor_scalar_mul(
             out=position_turns[:], in0=position[:], scalar1=1.0 / (2.0 * math.pi)
         )
+        minus_position = keep.tile([P, TILES], F32)
+        nc.vector.tensor_scalar_mul(out=minus_position[:], in0=position[:], scalar1=-1.0)
+        quarter_turn = keep.tile([P, 1], F32)
+        nc.vector.tensor_scalar_mul(out=quarter_turn[:], in0=freq[:, 0:1], scalar1=math.pi / 2)
 
         cos = keep.tile([P, TILES, HALF], F32)
         sin = keep.tile([P, TILES, HALF], F32)
 
-        turns = keep.tile([P, TILES, SLOW], F32)
-        shifted = keep.tile([P, TILES, SLOW], F32)
+        nearest = keep.tile([P, TILES, SLOW], I32)
         excess = keep.tile([P, TILES, SLOW], F32)
         for t in range(TILES):
             nc.vector.tensor_scalar_mul(
-                out=turns[:, t, :], in0=freq[:, :SLOW], scalar1=position_turns[:, t : t + 1]
-            )
-            nc.vector.tensor_scalar(
-                out=shifted[:, t, :],
-                in0=freq[:, :SLOW],
-                scalar1=position_turns[:, t : t + 1],
-                scalar2=ROUND,
-                op0=ALU.mult,
-                op1=ALU.add,
+                out=nearest[:, t, :], in0=freq[:, :SLOW], scalar1=position_turns[:, t : t + 1]
             )
         for t in range(TILES):
             nc.vector.scalar_tensor_tensor(
                 out=excess[:, t, :],
-                in0=shifted[:, t, :],
-                scalar=ROUND,
-                in1=turns[:, t, :],
-                op0=ALU.subtract,
+                in0=freq[:, :SLOW],
+                scalar=position_turns[:, t : t + 1],
+                in1=nearest[:, t, :],
+                op0=ALU.mult,
                 op1=ALU.subtract,
             )
 
@@ -121,10 +111,10 @@ def tile_ropeattention_pa_s_kernel(tc, x, w, grad_out, out):
                 scale=minus_position[:, t : t + 1],
                 bias=quarter_turn[:],
             )
-            nc.scalar.activation(
-                out=sin[:, t, :SLOW], in_=excess[:, t, :], func=ACT.Sin, scale=-2.0 * math.pi
-            )
             nc.scalar.activation(out=size[:, t, :], in_=excess[:, t, :], func=ACT.Abs)
+            nc.scalar.activation(
+                out=sin[:, t, :SLOW], in_=excess[:, t, :], func=ACT.Sin, scale=2.0 * math.pi
+            )
             nc.scalar.activation(
                 out=cos[:, t, :SLOW],
                 in_=size[:, t, :],
@@ -205,8 +195,9 @@ def tile_ropeattention_pa_s_kernel(tc, x, w, grad_out, out):
                 stop=True,
             )
             result = work.tile([P, D], F32)
-            if t % 2 == 0:
-                nc.scalar.copy(out=result[:], in_=acc[:])
-            else:
-                nc.vector.tensor_copy(out=result[:], in_=acc[:])
-            nc.sync.dma_start(out=out[t * P : (t + 1) * P, :], in_=result[:])
+            for half in (slice(0, D // 2), slice(D // 2, D)):
+                if t % 2 == 0:
+                    nc.scalar.copy(out=result[:, half], in_=acc[:, half])
+                else:
+                    nc.vector.tensor_copy(out=result[:, half], in_=acc[:, half])
+                nc.sync.dma_start(out=out[t * P : (t + 1) * P, half], in_=result[:, half])

@@ -85,11 +85,14 @@ def tile_ropeattention_pa_s_kernel(tc, x, w, grad_out, out):
 
         nearest = keep.tile([P, TILES, SLOW], I32)
         excess = keep.tile([P, TILES, SLOW], F32)
-        for t in range(TILES):
+        minus_size = keep.tile([P, TILES, SLOW], F32)
+
+        def make_nearest(t):
             nc.vector.tensor_scalar_mul(
                 out=nearest[:, t, :], in0=freq[:, :SLOW], scalar1=position_turns[:, t : t + 1]
             )
-        for t in range(TILES):
+
+        def make_excess(t):
             nc.vector.scalar_tensor_tensor(
                 out=excess[:, t, :],
                 in0=freq[:, :SLOW],
@@ -99,7 +102,29 @@ def tile_ropeattention_pa_s_kernel(tc, x, w, grad_out, out):
                 op1=ALU.subtract,
             )
 
-        size = keep.tile([P, TILES, SLOW], F32)
+        def make_minus_size(t):
+            nc.vector.scalar_tensor_tensor(
+                out=minus_size[:, t, :],
+                in0=excess[:, t, :],
+                scalar=-1.0,
+                in1=excess[:, t, :],
+                op0=ALU.mult,
+                op1=ALU.min,
+            )
+
+        make_nearest(0)
+        make_nearest(1)
+        make_excess(0)
+        make_nearest(2)
+        make_minus_size(0)
+        make_excess(1)
+        make_nearest(3)
+        make_minus_size(1)
+        make_excess(2)
+        make_excess(3)
+        make_minus_size(2)
+        make_minus_size(3)
+
         for t in range(TILES):
             nc.scalar.activation(
                 out=sin[:, t, SLOW:], in_=freq[:, SLOW:], func=ACT.Sin, scale=position[:, t : t + 1]
@@ -111,15 +136,14 @@ def tile_ropeattention_pa_s_kernel(tc, x, w, grad_out, out):
                 scale=minus_position[:, t : t + 1],
                 bias=quarter_turn[:],
             )
-            nc.scalar.activation(out=size[:, t, :], in_=excess[:, t, :], func=ACT.Abs)
             nc.scalar.activation(
                 out=sin[:, t, :SLOW], in_=excess[:, t, :], func=ACT.Sin, scale=2.0 * math.pi
             )
             nc.scalar.activation(
                 out=cos[:, t, :SLOW],
-                in_=size[:, t, :],
+                in_=minus_size[:, t, :],
                 func=ACT.Sin,
-                scale=-2.0 * math.pi,
+                scale=2.0 * math.pi,
                 bias=quarter_turn[:],
             )
 
@@ -132,26 +156,29 @@ def tile_ropeattention_pa_s_kernel(tc, x, w, grad_out, out):
         gy_grouped = keep.tile([P, TILES, P, PACK], BF16, align_bytes=64)
         for t in range(TILES):
             pairs = g_rows[:, t, :].rearrange("p (i e) -> p e i", e=2)
-            by_sin = work.tile([P, 2, HALF], F32)
+            by_sin_even = work.tile([P, HALF], F32)
             by_cos = work.tile([P, 2, HALF], F32)
-            nc.vector.tensor_mul(out=by_sin[:, 0, :], in0=pairs[:, 1, :], in1=sin[:, t, :])
-            nc.vector.tensor_mul(out=by_cos[:, 0, :], in0=pairs[:, 0, :], in1=cos[:, t, :])
+            by_sin_odd = work.tile([P, HALF], F32)
+            by_sin = [by_sin_even, by_sin_odd]
+            nc.vector.tensor_mul(out=by_sin_even[:], in0=pairs[:, 1, :], in1=sin[:, t, :])
+            nc.vector.tensor_mul(
+                out=by_cos[:], in0=pairs, in1=cos[:, t, :].unsqueeze(1).to_broadcast([P, 2, HALF])
+            )
             nc.vector.scalar_tensor_tensor(
-                out=by_sin[:, 1, :],
+                out=by_sin_odd[:],
                 in0=pairs[:, 0, :],
                 scalar=-1.0,
                 in1=sin[:, t, :],
                 op0=ALU.mult,
                 op1=ALU.mult,
             )
-            nc.vector.tensor_mul(out=by_cos[:, 1, :], in0=pairs[:, 1, :], in1=cos[:, t, :])
             flipped = flipped_pool.tile([P, PACK, P], F32)
             for e in range(2):
                 for u in range(2):
                     block = slice(u * P, (u + 1) * P)
                     nc.tensor.matmul(
                         out=flipped[:, 2 * u + e, :],
-                        lhsT=by_sin[:, e, block],
+                        lhsT=by_cos[:, e, block],
                         rhs=identity[:],
                         is_transpose=True,
                         start=True,
@@ -159,7 +186,7 @@ def tile_ropeattention_pa_s_kernel(tc, x, w, grad_out, out):
                     )
                     nc.tensor.matmul(
                         out=flipped[:, 2 * u + e, :],
-                        lhsT=by_cos[:, e, block],
+                        lhsT=by_sin[e][:, block],
                         rhs=identity[:],
                         is_transpose=True,
                         start=False,

@@ -148,10 +148,7 @@ def tile_ropeattention_pa_s_kernel(tc, x, w, grad_out, out):
             )
 
         w_grouped = keep.tile([P, D, PACK], BF16, align_bytes=64)
-        nc.scalar.copy(
-            out=w_grouped[:].rearrange("p (c i) q -> p c q i", i=4),
-            in_=w_rows[:].rearrange("p q (c i) -> p c q i", i=4),
-        )
+        nc.scalar.copy(out=w_grouped[:], in_=w_rows[:].rearrange("p q n -> p n q"))
 
         gy_grouped = keep.tile([P, TILES, P, PACK], BF16, align_bytes=64)
         for t in range(TILES):

@@ -71,6 +71,10 @@ def tile_ropeattention_pa_s_kernel(tc, x, w, grad_out, out):
                 )
             have *= 4
 
+        acc = acc_pool.tile([P, D], F32)
+        for repeat in range(3):
+            nc.tensor.matmul(out=acc[:, :HALF], lhsT=identity[:], rhs=freq[:], start=True, stop=True)
+
         position_turns = keep.tile([P, TILES], F32)
         nc.vector.tensor_scalar_mul(
             out=position_turns[:], in0=position[:], scalar1=1.0 / (2.0 * math.pi)

@@ -25,6 +25,8 @@ BASE = 10000.0
 SLOW = 144
 assert (S - 1) * BASE ** (-SLOW / HALF) < math.pi
 
+W_SCALAR = 384
+
 FLOPS = 2 * S * D * D
 BYTES = 2 * D * D + 2 * S * D + 4 * S * D
 
@@ -152,7 +154,9 @@ def tile_ropeattention_pa_s_kernel(tc, x, w, grad_out, out):
             )
 
         w_grouped = keep.tile([P, D, PACK], BF16, align_bytes=64)
-        nc.scalar.copy(out=w_grouped[:], in_=w_rows[:].rearrange("p q n -> p n q"))
+        nc.scalar.copy(
+            out=w_grouped[:, :W_SCALAR, :], in_=w_rows[:, :, :W_SCALAR].rearrange("p q n -> p n q")
+        )
 
         gy_grouped = keep.tile([P, TILES, P, PACK], BF16, align_bytes=64)
         for t in range(TILES):
@@ -194,6 +198,10 @@ def tile_ropeattention_pa_s_kernel(tc, x, w, grad_out, out):
                         stop=True,
                     )
             nc.scalar.copy(out=gy_grouped[:, t], in_=flipped[:].rearrange("p q j -> p j q"))
+
+        nc.vector.tensor_copy(
+            out=w_grouped[:, W_SCALAR:, :], in_=w_rows[:, :, W_SCALAR:].rearrange("p q n -> p n q")
+        )
 
         w_codes = keep.tile([P, D], U32, align_bytes=64)
         w_scales = keep.tile([P, D], U8, align_bytes=64)

@@ -22,8 +22,14 @@ HALF = D // 2
 TILES = S // P
 BASE = 10000.0
 
-SLOW = 144
-assert (S - 1) * BASE ** (-SLOW / HALF) < math.pi
+def first_slow_pair(last_position):
+    pair = 0
+    while last_position * BASE ** (-pair / HALF) >= math.pi:
+        pair += 8
+    return pair
+
+
+SLOW = [first_slow_pair((t + 1) * P - 1) for t in range(TILES)]
 
 W_SCALAR = 384
 
@@ -63,6 +69,14 @@ def tile_ropeattention_pa_s_kernel(tc, x, w, grad_out, out):
 
         freq = keep.tile([P, HALF], F32)
         nc.vector.memset(freq[:, 0:1], 1.0)
+        quarter_turn = keep.tile([P, 1], F32)
+        position_turns = keep.tile([P, TILES], F32)
+        minus_position = keep.tile([P, TILES], F32)
+        between_rounds = [
+            (quarter_turn[:], freq[:, 0:1], math.pi / 2),
+            (position_turns[:], position[:], 1.0 / (2.0 * math.pi)),
+            (minus_position[:], position[:], -1.0),
+        ]
         have = 1
         while have < HALF:
             for d in range(1, 4):
@@ -72,48 +86,43 @@ def tile_ropeattention_pa_s_kernel(tc, x, w, grad_out, out):
                     scalar1=BASE ** (-d * have / HALF),
                 )
             have *= 4
+            if between_rounds:
+                constant, source, factor = between_rounds.pop(0)
+                nc.vector.tensor_scalar_mul(out=constant, in0=source, scalar1=factor)
 
         acc = acc_pool.tile([P, D], F32)
         for repeat in range(3):
             nc.tensor.matmul(out=acc[:, :HALF], lhsT=identity[:], rhs=freq[:], start=True, stop=True)
 
-        position_turns = keep.tile([P, TILES], F32)
-        nc.vector.tensor_scalar_mul(
-            out=position_turns[:], in0=position[:], scalar1=1.0 / (2.0 * math.pi)
-        )
-        minus_position = keep.tile([P, TILES], F32)
-        nc.vector.tensor_scalar_mul(out=minus_position[:], in0=position[:], scalar1=-1.0)
-        quarter_turn = keep.tile([P, 1], F32)
-        nc.vector.tensor_scalar_mul(out=quarter_turn[:], in0=freq[:, 0:1], scalar1=math.pi / 2)
 
         cos = keep.tile([P, TILES, HALF], F32)
         sin = keep.tile([P, TILES, HALF], F32)
 
-        nearest = keep.tile([P, TILES, SLOW], I32)
-        excess = keep.tile([P, TILES, SLOW], F32)
-        minus_size = keep.tile([P, TILES, SLOW], F32)
+        nearest = keep.tile([P, TILES, max(SLOW)], I32)
+        excess = keep.tile([P, TILES, max(SLOW)], F32)
+        minus_size = keep.tile([P, TILES, max(SLOW)], F32)
 
         def make_nearest(t):
             nc.vector.tensor_scalar_mul(
-                out=nearest[:, t, :], in0=freq[:, :SLOW], scalar1=position_turns[:, t : t + 1]
+                out=nearest[:, t, : SLOW[t]], in0=freq[:, : SLOW[t]], scalar1=position_turns[:, t : t + 1]
             )
 
         def make_excess(t):
             nc.vector.scalar_tensor_tensor(
-                out=excess[:, t, :],
-                in0=freq[:, :SLOW],
+                out=excess[:, t, : SLOW[t]],
+                in0=freq[:, : SLOW[t]],
                 scalar=position_turns[:, t : t + 1],
-                in1=nearest[:, t, :],
+                in1=nearest[:, t, : SLOW[t]],
                 op0=ALU.mult,
                 op1=ALU.subtract,
             )
 
         def make_minus_size(t):
             nc.vector.scalar_tensor_tensor(
-                out=minus_size[:, t, :],
-                in0=excess[:, t, :],
+                out=minus_size[:, t, : SLOW[t]],
+                in0=excess[:, t, : SLOW[t]],
                 scalar=-1.0,
-                in1=excess[:, t, :],
+                in1=excess[:, t, : SLOW[t]],
                 op0=ALU.mult,
                 op1=ALU.min,
             )
@@ -133,21 +142,21 @@ def tile_ropeattention_pa_s_kernel(tc, x, w, grad_out, out):
 
         for t in range(TILES):
             nc.scalar.activation(
-                out=sin[:, t, SLOW:], in_=freq[:, SLOW:], func=ACT.Sin, scale=position[:, t : t + 1]
+                out=sin[:, t, SLOW[t] :], in_=freq[:, SLOW[t] :], func=ACT.Sin, scale=position[:, t : t + 1]
             )
             nc.scalar.activation(
-                out=cos[:, t, SLOW:],
-                in_=freq[:, SLOW:],
+                out=cos[:, t, SLOW[t] :],
+                in_=freq[:, SLOW[t] :],
                 func=ACT.Sin,
                 scale=minus_position[:, t : t + 1],
                 bias=quarter_turn[:],
             )
             nc.scalar.activation(
-                out=sin[:, t, :SLOW], in_=excess[:, t, :], func=ACT.Sin, scale=2.0 * math.pi
+                out=sin[:, t, : SLOW[t]], in_=excess[:, t, : SLOW[t]], func=ACT.Sin, scale=2.0 * math.pi
             )
             nc.scalar.activation(
-                out=cos[:, t, :SLOW],
-                in_=minus_size[:, t, :],
+                out=cos[:, t, : SLOW[t]],
+                in_=minus_size[:, t, : SLOW[t]],
                 func=ACT.Sin,
                 scale=2.0 * math.pi,
                 bias=quarter_turn[:],
@@ -169,14 +178,17 @@ def tile_ropeattention_pa_s_kernel(tc, x, w, grad_out, out):
             nc.vector.tensor_mul(
                 out=by_cos[:], in0=pairs, in1=cos[:, t, :].unsqueeze(1).to_broadcast([P, 2, HALF])
             )
-            nc.vector.scalar_tensor_tensor(
-                out=by_sin_odd[:],
-                in0=pairs[:, 0, :],
-                scalar=-1.0,
-                in1=sin[:, t, :],
-                op0=ALU.mult,
-                op1=ALU.mult,
-            )
+            pieces = 2 if t == TILES - 1 else 1
+            for piece in range(pieces):
+                part = slice(piece * HALF // pieces, (piece + 1) * HALF // pieces)
+                nc.vector.scalar_tensor_tensor(
+                    out=by_sin_odd[:, part],
+                    in0=pairs[:, 0, part],
+                    scalar=-1.0,
+                    in1=sin[:, t, part],
+                    op0=ALU.mult,
+                    op1=ALU.mult,
+                )
             flipped = flipped_pool.tile([P, PACK, P], F32)
             for e in range(2):
                 for u in range(2):

@@ -31,8 +31,6 @@ def first_slow_pair(last_position):
 
 SLOW = [first_slow_pair((t + 1) * P - 1) for t in range(TILES)]
 
-W_SCALAR = 384
-
 FLOPS = 2 * S * D * D
 BYTES = 2 * D * D + 2 * S * D + 4 * S * D
 
@@ -163,9 +161,7 @@ def tile_ropeattention_pa_s_kernel(tc, x, w, grad_out, out):
             )
 
         w_grouped = keep.tile([P, D, PACK], BF16, align_bytes=64)
-        nc.scalar.copy(
-            out=w_grouped[:, :W_SCALAR, :], in_=w_rows[:, :, :W_SCALAR].rearrange("p q n -> p n q")
-        )
+        nc.scalar.copy(out=w_grouped[:], in_=w_rows[:].rearrange("p q n -> p n q"))
 
         gy_grouped = keep.tile([P, TILES, P, PACK], BF16, align_bytes=64)
         for t in range(TILES):
@@ -210,10 +206,6 @@ def tile_ropeattention_pa_s_kernel(tc, x, w, grad_out, out):
                         stop=True,
                     )
             nc.scalar.copy(out=gy_grouped[:, t], in_=flipped[:].rearrange("p q j -> p j q"))
-
-        nc.vector.tensor_copy(
-            out=w_grouped[:, W_SCALAR:, :], in_=w_rows[:, :, W_SCALAR:].rearrange("p q n -> p n q")
-        )
 
         w_codes = keep.tile([P, D], U32, align_bytes=64)
         w_scales = keep.tile([P, D], U8, align_bytes=64)

@@ -89,8 +89,9 @@ def tile_ropeattention_pa_s_kernel(tc, x, w, grad_out, out):
                 nc.vector.tensor_scalar_mul(out=constant, in0=source, scalar1=factor)
 
         acc = acc_pool.tile([P, D], F32)
+        unread = acc
         for repeat in range(3):
-            nc.tensor.matmul(out=acc[:, :HALF], lhsT=identity[:], rhs=freq[:], start=True, stop=True)
+            nc.tensor.matmul(out=unread[:, :HALF], lhsT=identity[:], rhs=freq[:], start=True, stop=True)
 
 
         cos = keep.tile([P, TILES, HALF], F32)
@@ -205,6 +206,15 @@ def tile_ropeattention_pa_s_kernel(tc, x, w, grad_out, out):
                         start=False,
                         stop=True,
                     )
+            for repeat in range(3):
+                nc.tensor.matmul(
+                    out=unread[:, :P],
+                    lhsT=identity[:],
+                    rhs=identity[:],
+                    is_transpose=True,
+                    start=True,
+                    stop=True,
+                )
             nc.scalar.copy(out=gy_grouped[:, t], in_=flipped[:].rearrange("p q j -> p j q"))
 
         w_codes = keep.tile([P, D], U32, align_bytes=64)

import math
from contextlib import ExitStack

import concourse.mybir as mybir
from concourse.masks import make_identity

F32 = mybir.dt.float32
BF16 = mybir.dt.bfloat16
I32 = mybir.dt.int32
U32 = mybir.dt.uint32
U8 = mybir.dt.uint8
E4M3_X4 = mybir.dt.float8_e4m3fn_x4
E5M2_X4 = mybir.dt.float8_e5m2_x4
ALU = mybir.AluOpType
ACT = mybir.ActivationFunctionType

S = 512
D = 512
P = 128
PACK = 4
HALF = D // 2
TILES = S // P
BASE = 10000.0

def first_slow_pair(last_position):
    pair = 0
    while last_position * BASE ** (-pair / HALF) >= math.pi:
        pair += 8
    return pair


SLOW = [first_slow_pair((t + 1) * P - 1) for t in range(TILES)]

FLOPS = 2 * S * D * D
BYTES = 2 * D * D + 2 * S * D + 4 * S * D


def tile_ropeattention_pa_s_kernel(tc, x, w, grad_out, out):
    nc = tc.nc
    with ExitStack() as ctx:
        ctx.enter_context(tc.manual_schedule())
        keep = ctx.enter_context(tc.tile_pool(name="keep", bufs=1))
        work = ctx.enter_context(tc.tile_pool(name="work", bufs=TILES))
        flipped_pool = ctx.enter_context(tc.psum_pool(name="flipped", bufs=TILES))
        acc_pool = ctx.enter_context(tc.psum_pool(name="acc", bufs=TILES))

        g_rows = keep.tile([P, TILES, D], BF16)
        w_rows = keep.tile([P, PACK, D], BF16)

        for t in range(TILES):
            nc.sync.dma_start(out=g_rows[:, t, :], in_=grad_out[t * P : (t + 1) * P, :])
        nc.sync.dma_start(
            out=w_rows[:].rearrange("p (u e) n -> p u e n", u=2),
            in_=w.rearrange("(u p e) n -> p u e n", u=2, e=2),
        )

        position = keep.tile([P, TILES], F32)
        nc.gpsimd.iota(
            position[:],
            pattern=[[P, TILES]],
            base=0,
            channel_multiplier=1,
            allow_small_or_imprecise_dtypes=True,
        )
        identity = keep.tile([P, P], F32)
        make_identity(nc, identity[:])

        freq = keep.tile([P, HALF], F32)
        nc.vector.memset(freq[:, 0:1], 1.0)
        quarter_turn = keep.tile([P, 1], F32)
        position_turns = keep.tile([P, TILES], F32)
        minus_position = keep.tile([P, TILES], F32)
        between_rounds = [
            (quarter_turn[:], freq[:, 0:1], math.pi / 2),
            (position_turns[:], position[:], 1.0 / (2.0 * math.pi)),
            (minus_position[:], position[:], -1.0),
        ]
        have = 1
        while have < HALF:
            for d in range(1, 4):
                nc.vector.tensor_scalar_mul(
                    out=freq[:, d * have : (d + 1) * have],
                    in0=freq[:, 0:have],
                    scalar1=BASE ** (-d * have / HALF),
                )
            have *= 4
            if between_rounds:
                constant, source, factor = between_rounds.pop(0)
                nc.vector.tensor_scalar_mul(out=constant, in0=source, scalar1=factor)

        acc = acc_pool.tile([P, D], F32)
        unread = acc
        for repeat in range(3):
            nc.tensor.matmul(out=unread[:, :HALF], lhsT=identity[:], rhs=freq[:], start=True, stop=True)


        cos = keep.tile([P, TILES, HALF], F32)
        sin = keep.tile([P, TILES, HALF], F32)

        nearest = keep.tile([P, TILES, max(SLOW)], I32)
        excess = keep.tile([P, TILES, max(SLOW)], F32)
        minus_size = keep.tile([P, TILES, max(SLOW)], F32)

        def make_nearest(t):
            nc.vector.tensor_scalar_mul(
                out=nearest[:, t, : SLOW[t]], in0=freq[:, : SLOW[t]], scalar1=position_turns[:, t : t + 1]
            )

        def make_excess(t):
            nc.vector.scalar_tensor_tensor(
                out=excess[:, t, : SLOW[t]],
                in0=freq[:, : SLOW[t]],
                scalar=position_turns[:, t : t + 1],
                in1=nearest[:, t, : SLOW[t]],
                op0=ALU.mult,
                op1=ALU.subtract,
            )

        def make_minus_size(t):
            nc.vector.scalar_tensor_tensor(
                out=minus_size[:, t, : SLOW[t]],
                in0=excess[:, t, : SLOW[t]],
                scalar=-1.0,
                in1=excess[:, t, : SLOW[t]],
                op0=ALU.mult,
                op1=ALU.min,
            )

        make_nearest(0)
        make_nearest(1)
        make_excess(0)
        make_nearest(2)
        make_minus_size(0)
        make_excess(1)
        make_nearest(3)
        make_minus_size(1)
        make_excess(2)
        make_excess(3)
        make_minus_size(2)
        make_minus_size(3)

        for t in range(TILES):
            nc.scalar.activation(
                out=sin[:, t, SLOW[t] :], in_=freq[:, SLOW[t] :], func=ACT.Sin, scale=position[:, t : t + 1]
            )
            nc.scalar.activation(
                out=cos[:, t, SLOW[t] :],
                in_=freq[:, SLOW[t] :],
                func=ACT.Sin,
                scale=minus_position[:, t : t + 1],
                bias=quarter_turn[:],
            )
            nc.scalar.activation(
                out=sin[:, t, : SLOW[t]], in_=excess[:, t, : SLOW[t]], func=ACT.Sin, scale=2.0 * math.pi
            )
            nc.scalar.activation(
                out=cos[:, t, : SLOW[t]],
                in_=minus_size[:, t, : SLOW[t]],
                func=ACT.Sin,
                scale=2.0 * math.pi,
                bias=quarter_turn[:],
            )

        w_grouped = keep.tile([P, D, PACK], BF16, align_bytes=64)
        nc.scalar.copy(out=w_grouped[:], in_=w_rows[:].rearrange("p q n -> p n q"))

        gy_grouped = keep.tile([P, TILES, P, PACK], BF16, align_bytes=64)
        for t in range(TILES):
            pairs = g_rows[:, t, :].rearrange("p (i e) -> p e i", e=2)
            by_sin_even = work.tile([P, HALF], F32)
            by_cos = work.tile([P, 2, HALF], F32)
            by_sin_odd = work.tile([P, HALF], F32)
            by_sin = [by_sin_even, by_sin_odd]
            nc.vector.tensor_mul(out=by_sin_even[:], in0=pairs[:, 1, :], in1=sin[:, t, :])
            nc.vector.tensor_mul(
                out=by_cos[:], in0=pairs, in1=cos[:, t, :].unsqueeze(1).to_broadcast([P, 2, HALF])
            )
            pieces = 2 if t == TILES - 1 else 1
            for piece in range(pieces):
                part = slice(piece * HALF // pieces, (piece + 1) * HALF // pieces)
                nc.vector.scalar_tensor_tensor(
                    out=by_sin_odd[:, part],
                    in0=pairs[:, 0, part],
                    scalar=-1.0,
                    in1=sin[:, t, part],
                    op0=ALU.mult,
                    op1=ALU.mult,
                )
            flipped = flipped_pool.tile([P, PACK, P], F32)
            for e in range(2):
                for u in range(2):
                    block = slice(u * P, (u + 1) * P)
                    nc.tensor.matmul(
                        out=flipped[:, 2 * u + e, :],
                        lhsT=by_cos[:, e, block],
                        rhs=identity[:],
                        is_transpose=True,
                        start=True,
                        stop=False,
                    )
                    nc.tensor.matmul(
                        out=flipped[:, 2 * u + e, :],
                        lhsT=by_sin[e][:, block],
                        rhs=identity[:],
                        is_transpose=True,
                        start=False,
                        stop=True,
                    )
            for repeat in range(3):
                nc.tensor.matmul(
                    out=unread[:, :P],
                    lhsT=identity[:],
                    rhs=identity[:],
                    is_transpose=True,
                    start=True,
                    stop=True,
                )
            nc.scalar.copy(out=gy_grouped[:, t], in_=flipped[:].rearrange("p q j -> p j q"))

        w_codes = keep.tile([P, D], U32, align_bytes=64)
        w_scales = keep.tile([P, D], U8, align_bytes=64)
        nc.vector.quantize_mx(
            out=w_codes[:].bitcast(E4M3_X4),
            scales=w_scales[:],
            in_=w_grouped[:].rearrange("p n q -> p (n q)"),
        )
        gy_codes = keep.tile([P, TILES, P], U32, align_bytes=64)
        gy_scales = keep.tile([P, TILES, P], U8, align_bytes=64)
        for t in range(TILES):
            nc.vector.quantize_mx(
                out=gy_codes[:, t, :].bitcast(E5M2_X4),
                scales=gy_scales[:, t, :],
                in_=gy_grouped[:, t].rearrange("p j q -> p (j q)"),
            )

        for t in range(TILES):
            acc = acc_pool.tile([P, D], F32)
            nc.tensor.matmul_mx(
                out=acc[:],
                lhsT=gy_codes[:, t, :].bitcast(E5M2_X4),
                lhsT_scale=gy_scales[:, t, :],
                rhs=w_codes[:].bitcast(E4M3_X4),
                rhs_scale=w_scales[:],
                start=True,
                stop=True,
            )
            result = work.tile([P, D], F32)
            for half in (slice(0, D // 2), slice(D // 2, D)):
                if t % 2 == 0:
                    nc.scalar.copy(out=result[:, half], in_=acc[:, half])
                else:
                    nc.vector.tensor_copy(out=result[:, half], in_=acc[:, half])
                nc.sync.dma_start(out=out[t * P : (t + 1) * P, half], in_=result[:, half])
